import numpy as np
import ml_dtypes


def mxq(x, axis, fmt="e4m3"):
    dtype, down = {"e4m3": (ml_dtypes.float8_e4m3fn, 7), "e5m2": (ml_dtypes.float8_e5m2, 14)}[fmt]
    v = np.moveaxis(np.asarray(x, np.float32).astype(ml_dtypes.bfloat16).astype(np.float64), axis, -1)
    blocks = v.reshape(v.shape[:-1] + (-1, 32))
    amax = np.abs(blocks).max(-1, keepdims=True)
    byte = np.maximum(np.where(amax > 0, np.frexp(amax)[1] - 1 + 127, 0) - down, 1)
    scale = np.exp2(byte - 127.0)
    codes = (blocks / scale).astype(np.float32).astype(dtype).astype(np.float64)
    return np.moveaxis((codes * scale).reshape(v.shape), -1, axis)


WIDE = False


def mx_kscale(k):
    if not WIDE:
        return np.ones(k)
    levels = np.array([10, -10, 5, -5, 0])
    a = np.random.permutation(np.resize(levels, k // 512 * 4)).reshape(k // 512, 4)
    idx = np.arange(k)
    return np.exp2(a[idx // 512, idx % 128 // 32])


BF16 = ml_dtypes.bfloat16


def bf(x):
    return np.asarray(x, np.float32).astype(BF16)


def f64(x):
    return np.asarray(x).astype(np.float64)


E2M1 = np.array([0.0, 0.5, 1.0, 1.5, 2.0, 3.0, 4.0, 6.0, -0.0, -0.5, -1.0, -1.5, -2.0, -3.0, -4.0, -6.0])


def pack_weight(w, fmt):
    k, n = w.shape
    w = f64(bf(w)).reshape(k // 32, 32, n)
    amax = np.abs(w).max(1)
    if fmt == "e4m3":
        byte = np.frexp(amax)[1] - 1 + 127 - 7
    else:
        mant, ex = np.frexp(amax / 6.0)
        byte = np.where(mant > 0.5, ex, ex - 1) + 127
    byte = np.clip(np.where(amax > 0, byte, 1), 1, 254)
    scaled = (w * np.exp2(127.0 - byte)[:, None, :]).reshape(k, n).astype(np.float32)
    by_word = np.ascontiguousarray(scaled.reshape(k // 512, 128, 4, n).transpose(0, 1, 3, 2))
    if fmt == "e4m3":
        words = by_word.astype(ml_dtypes.float8_e4m3fn).view(np.uint8)
    else:
        c = by_word.astype(ml_dtypes.float4_e2m1fn).view(np.uint8) & 0xF
        words = c[..., 0::2] | (c[..., 1::2] << 4)
    return np.ascontiguousarray(words), np.ascontiguousarray(byte.astype(np.uint8).reshape(k // 512, 16, n))


def unpack_weight(words, scales, fmt):
    g, p, n, _ = words.shape
    if fmt == "e4m3":
        vals = np.ascontiguousarray(words).view(ml_dtypes.float8_e4m3fn).astype(np.float64)
    else:
        nib = np.empty((g, p, n, 4), np.uint8)
        nib[..., 0::2] = words & 0xF
        nib[..., 1::2] = words >> 4
        vals = E2M1[nib]
    vals = vals * np.repeat(np.exp2(scales.astype(np.float64) - 127.0), 8, axis=1)[..., None]
    return vals.transpose(0, 1, 3, 2).reshape(g * 512, n)


B, D_IN, D_HID, SHARE = 128, 8192, 384, 2
NUM_GATE = 4 + SHARE


def sigmoid(v):
    return 1.0 / (1.0 + np.exp(-v))


def setup_inputs():
    s = mx_kscale(D_IN)
    n = np.random.standard_normal
    inp = bf(n((B, D_IN)) * s)
    h_minors = bf(n((B, D_HID)))
    c_minors = bf(n((B, D_HID)))
    s_minors = bf(n((SHARE, B, D_HID)))
    mask = bf(np.random.uniform(0.5, 1.5, B))
    w_ih = n((NUM_GATE * D_HID, D_IN)) * 0.7 / np.sqrt(D_IN) / s
    words, scales = pack_weight(np.ascontiguousarray(w_ih.T), "e4m3")
    return {
        "input": inp,
        "h_minors": h_minors,
        "c_minors": c_minors,
        "s_minors": s_minors,
        "mask": mask,
        "weight_ih_words": words,
        "weight_ih_scales": scales,
        "weight_hh": bf(n((4 * D_HID, D_HID)) * 0.7 / np.sqrt(D_HID)),
        "weight_sh": bf(n((SHARE * D_HID, D_HID)) * 0.7 / np.sqrt(D_HID)),
        "bias_ih": bf(n(NUM_GATE * D_HID) * 0.3),
        "bias_hh": bf(n(4 * D_HID) * 0.3),
        "bias_sh": bf(n(SHARE * D_HID) * 0.3),
        "idx": 0,
    }


def reference(input, h_minors, c_minors, s_minors, mask, weight_ih_words, weight_ih_scales, weight_hh, weight_sh, bias_ih, bias_hh, bias_sh, idx):
    H = weight_hh.shape[1]
    share = weight_sh.shape[0] // H
    m = f64(mask)[:, None]
    tmp = (mxq(f64(input), 1, "e4m3") @ unpack_weight(weight_ih_words, weight_ih_scales, "e4m3")) + f64(bias_ih)
    tmp2 = f64(h_minors) @ f64(weight_hh).T + f64(bias_hh)
    tmp3 = f64(s_minors)[idx] @ f64(weight_sh).T + f64(bias_sh)
    tmp_in, tmp_s = tmp[:, :4 * H], tmp[:, 4 * H:]
    z = tmp_in + tmp2
    ifo = sigmoid(z[:, :3 * H])
    i, f, o = ifo[:, :H], ifo[:, H:2 * H], ifo[:, 2 * H:]
    c_hat = z[:, 3 * H:]
    b = sigmoid(tmp_s + tmp3)
    c_t = (f * f64(c_minors) + i * np.tanh(c_hat)) * m
    tc = np.tanh(c_t) * m
    h = o * tc
    s = b.reshape(-1, share, H) * tc[:, None, :]
    s = np.moveaxis(s, 1, 0)
    return (h, c_t, s[0], s[1])

@@ -1,0 +1,328 @@
+from contextlib import ExitStack
+
+import concourse.mybir as mybir
+from concourse.masks import make_identity
+
+F32 = mybir.dt.float32
+BF16 = mybir.dt.bfloat16
+I32 = mybir.dt.int32
+U32 = mybir.dt.uint32
+U8 = mybir.dt.uint8
+FP8X4 = mybir.dt.float8_e4m3fn_x4
+ACT = mybir.ActivationFunctionType
+ALU = mybir.AluOpType
+
+P = 128
+D_IN = 8192
+H = 384
+N_CELL = 4 * H
+N_ALL = 6 * H
+K_PASS = 4 * P
+PASSES = D_IN // K_PASS
+H_CHUNKS = H // P
+BANK = 512
+ALL_BANKS = range(0, 5)
+CELL_BANKS = range(0, 3)
+SHARE_BANKS = range(3, 5)
+PLANES_PER_TILE = 4
+X_PIECES = 4
+PASSES_PER_PIECE = PASSES // X_PIECES
+SPLIT_PASSES = 6
+W_BUFS = 11
+
+FLOPS = 2 * P * (D_IN * N_ALL + H * N_ALL)
+BYTES = (
+    2 * P * D_IN + 3 * 2 * P * H + 2 * P + D_IN * N_ALL + D_IN // 32 * N_ALL
+    + 2 * N_ALL * H + 2 * 2 * N_ALL + 4 * 4 * P * H
+)
+
+
+def bank_columns(banks):
+    return banks[0] * BANK, min((banks[-1] + 1) * BANK, N_ALL)
+
+
+def copy_out(nc, turn, out, in_):
+    if turn % 2 == 0:
+        nc.vector.tensor_copy(out=out, in_=in_)
+    else:
+        nc.scalar.copy(out=out, in_=in_)
+
+
+def tile_share_lstm_cell_w_kernel(
+    tc, x, h_minors, c_minors, s_minors, mask, weight_ih_words, weight_ih_scales,
+    weight_hh, weight_sh, bias_ih, bias_hh, bias_sh, idx, out_0, out_1, out_2, out_3,
+):
+    nc = tc.nc
+    with ExitStack() as stack:
+        keep = stack.enter_context(tc.tile_pool(name="keep", bufs=1))
+        w_pool = stack.enter_context(tc.tile_pool(name="w_pool", bufs=W_BUFS))
+        acc_pool = stack.enter_context(tc.psum_pool(name="acc_pool", bufs=1))
+        work = stack.enter_context(tc.psum_pool(name="work", bufs=3))
+        stack.enter_context(tc.manual_schedule())
+
+        warm = keep.tile([P, 1], F32)
+        nc.vector.memset(warm[:], 0.0)
+        nc.scalar.activation(out=warm[:], in_=warm[:], func=ACT.Sigmoid)
+
+        ident_f32 = keep.tile([P, P], F32)
+        make_identity(nc, ident_f32[:])
+        ident_bf16 = keep.tile([P, P], BF16)
+        make_identity(nc, ident_bf16[:])
+        ones = keep.tile([P, P], BF16)
+        nc.vector.memset(ones[:], 1.0)
+
+        bias_rows = keep.tile([P, N_ALL], BF16)
+        nc.vector.memset(bias_rows[:], 0.0)
+
+        w_planes = keep.tile([P, PASSES // PLANES_PER_TILE, N_ALL], U8, align_bytes=64)
+        nc.vector.memset(w_planes[:].bitcast(I32), 0)
+
+        hs_raw = keep.tile([P, 2, H], BF16)
+        nc.gpsimd.dma_start(out=hs_raw[:, 0, :], in_=h_minors)
+        nc.gpsimd.dma_start(out=hs_raw[:, 1, :], in_=s_minors[idx])
+        nc.gpsimd.dma_start(out=bias_rows[0:1, :], in_=bias_ih.rearrange("(o n) -> o n", o=1))
+        nc.gpsimd.dma_start(
+            out=bias_rows[1:2, 0:N_CELL], in_=bias_hh.rearrange("(o n) -> o n", o=1)
+        )
+        nc.gpsimd.dma_start(
+            out=bias_rows[1:2, N_CELL:N_ALL], in_=bias_sh.rearrange("(o n) -> o n", o=1)
+        )
+        c_prev = keep.tile([P, H], BF16)
+        nc.gpsimd.dma_start(out=c_prev[:], in_=c_minors)
+        mask_bf16 = keep.tile([P, 1], BF16)
+        nc.gpsimd.dma_start(out=mask_bf16[:], in_=mask.rearrange("(p o) -> p o", o=1))
+
+        x_sb = keep.tile([P, D_IN], BF16)
+        x_cols = D_IN // X_PIECES
+        for piece in range(X_PIECES):
+            cols = slice(piece * x_cols, (piece + 1) * x_cols)
+            nc.sync.dma_start(out=x_sb[:, cols], in_=x[:, cols])
+
+        w_raw = keep.tile([P, N_ALL // P, H], BF16)
+        for b in ALL_BANKS:
+            first, last = bank_columns(range(b, b + 1))
+            rows_each = (last - first) // P
+            if last <= N_CELL:
+                rows = weight_hh[first:last, :]
+            else:
+                rows = weight_sh[first - N_CELL : last - N_CELL, :]
+            nc.sync.dma_start(
+                out=w_raw[:, first // P : last // P, :],
+                in_=rows.rearrange("(p j) k -> p j k", j=rows_each),
+            )
+
+        for tile_no in range(PASSES // PLANES_PER_TILE):
+            g0 = tile_no * PLANES_PER_TILE
+            for quad in range(4):
+                nc.sync.dma_start(
+                    out=w_planes[32 * quad : 32 * quad + 16, tile_no, :].bitcast(I32),
+                    in_=weight_ih_scales[
+                        g0 : g0 + PLANES_PER_TILE, 4 * quad : 4 * quad + 4, :
+                    ].bitcast(I32),
+                )
+
+        whole = range(PASSES - SPLIT_PASSES)
+        split = range(PASSES - SPLIT_PASSES, PASSES)
+        pieces = [(g, ALL_BANKS) for g in whole]
+        pieces += [(g, CELL_BANKS) for g in split]
+        pieces += [(g, SHARE_BANKS) for g in split]
+        w_words = {}
+
+        def load_piece(g, banks):
+            if g not in w_words:
+                w_words[g] = w_pool.tile(
+                    [P, N_ALL], U32, name="w_words_%d" % g, tag="w_words", align_bytes=64
+                )
+            first, last = bank_columns(banks)
+            nc.sync.dma_start(
+                out=w_words[g][:, first:last].bitcast(I32),
+                in_=weight_ih_words[g]
+                .rearrange("p n t -> p (n t)")[:, 4 * first : 4 * last]
+                .bitcast(I32),
+            )
+
+        for g, banks in pieces[:W_BUFS]:
+            load_piece(g, banks)
+
+        x_words = x_sb[:].bitcast(F32)
+        words_per_pass = K_PASS // 2
+        x_grouped = keep.tile([P, PASSES * P * 4], BF16, align_bytes=64)
+        x_grouped_words = x_grouped[:].bitcast(F32).rearrange(
+            "p (g r u) -> p g r u", g=PASSES, u=2
+        )
+        x_codes = keep.tile([P, PASSES * P], U32, align_bytes=64)
+        x_scales = keep.tile([P, PASSES * P], U8, align_bytes=64)
+
+        def quantise_piece(piece):
+            first = piece * PASSES_PER_PIECE * P
+            last = first + PASSES_PER_PIECE * P
+            nc.vector.quantize_mx(
+                out=x_codes[:, first:last].bitcast(FP8X4),
+                scales=x_scales[:, first:last],
+                in_=x_grouped[:, 4 * first : 4 * last],
+            )
+
+        for piece in range(X_PIECES):
+            for half in range(PASSES_PER_PIECE // 2):
+                g0 = piece * PASSES_PER_PIECE + 2 * half
+                x_t = work.tile([P, 2, 2, P], F32, tag="work")
+                for i in range(2):
+                    for u in range(2):
+                        start_word = (g0 + i) * words_per_pass
+                        nc.tensor.transpose(
+                            x_t[:, i, u, :],
+                            x_words[:, start_word + u : start_word + words_per_pass : 2],
+                            ident_f32[:],
+                        )
+                copy_out(
+                    nc, half,
+                    out=x_grouped_words[:, g0 : g0 + 2, :, :],
+                    in_=x_t[:].rearrange("p i u r -> p i r u"),
+                )
+            if piece > 0:
+                quantise_piece(piece - 1)
+        quantise_piece(X_PIECES - 1)
+
+        hs_t = keep.tile([P, 2, H_CHUNKS, P], BF16)
+        for side in range(2):
+            h_t = work.tile([P, H_CHUNKS, P], BF16, tag="work")
+            for kc in range(H_CHUNKS):
+                nc.tensor.transpose(
+                    h_t[:, kc, :], hs_raw[:, side, kc * P : (kc + 1) * P], ident_bf16[:]
+                )
+            copy_out(nc, side, out=hs_t[:, side, :, :], in_=h_t[:])
+
+        w_t = keep.tile([P, H_CHUNKS, N_ALL], BF16)
+
+        def transpose_plain_weights(b):
+            first, last = bank_columns(range(b, b + 1))
+            rows_each = (last - first) // P
+            for kc in range(H_CHUNKS):
+                block_t = work.tile([P, rows_each, P], BF16, tag="work")
+                for j in range(rows_each):
+                    nc.tensor.transpose(
+                        block_t[:, j, :],
+                        w_raw[:, first // P + j, kc * P : (kc + 1) * P],
+                        ident_bf16[:],
+                    )
+                copy_out(
+                    nc, b + kc,
+                    out=w_t[:, kc, first:last].rearrange("k (p j) -> k p j", j=rows_each),
+                    in_=block_t[:].rearrange("k j p -> k p j"),
+                )
+
+        plain_sum = keep.tile([P, N_ALL], F32)
+
+        def plain_products(b):
+            first, last = bank_columns(range(b, b + 1))
+            side = 0 if last <= N_CELL else 1
+            plain_ps = work.tile([P, last - first], F32, tag="work")
+            for kc in range(H_CHUNKS):
+                nc.tensor.matmul(
+                    plain_ps[:], lhsT=hs_t[:, side, kc, :], rhs=w_t[:, kc, first:last],
+                    start=(kc == 0), stop=False,
+                )
+            nc.tensor.matmul(
+                plain_ps[:], lhsT=ones[:], rhs=bias_rows[:, first:last], start=False, stop=True
+            )
+            copy_out(nc, b, out=plain_sum[:, first:last], in_=plain_ps[:])
+
+        transpose_plain_weights(0)
+        for b in ALL_BANKS:
+            if b + 1 < len(ALL_BANKS):
+                transpose_plain_weights(b + 1)
+            plain_products(b)
+
+        mask_f32 = keep.tile([P, 1], F32)
+        nc.vector.tensor_copy(out=mask_f32[:], in_=mask_bf16[:])
+
+        acc = []
+        for b in ALL_BANKS:
+            first, last = bank_columns(range(b, b + 1))
+            acc.append(acc_pool.tile([P, last - first], F32, name="acc%d" % b))
+
+        def multiply_piece(g, banks):
+            offset = 4 * (g % PLANES_PER_TILE)
+            for b in banks:
+                first, last = bank_columns(range(b, b + 1))
+                nc.tensor.matmul_mx(
+                    out=acc[b][:],
+                    lhsT=x_codes[:, g * P : (g + 1) * P].bitcast(FP8X4),
+                    lhsT_scale=x_scales[:, g * P : (g + 1) * P],
+                    rhs=w_words[g][:, first:last].bitcast(FP8X4),
+                    rhs_scale=w_planes[offset:P, g // PLANES_PER_TILE, first:last],
+                    start=(g == 0),
+                    stop=(g == PASSES - 1),
+                )
+
+        gates = keep.tile([P, N_ALL], F32)
+
+        def add_plain_sum(b):
+            first, last = bank_columns(range(b, b + 1))
+            nc.vector.tensor_tensor(
+                out=gates[:, first:last], in0=acc[b][:], in1=plain_sum[:, first:last], op=ALU.add
+            )
+
+        def activate(first, last, func):
+            nc.scalar.activation(out=gates[:, first:last], in_=gates[:, first:last], func=func)
+
+        def multiply_and_load_ahead(n):
+            multiply_piece(*pieces[n])
+            if n + W_BUFS < len(pieces):
+                load_piece(*pieces[n + W_BUFS])
+
+        for n in range(PASSES):
+            multiply_and_load_ahead(n)
+
+        for b in CELL_BANKS:
+            add_plain_sum(b)
+        activate(0, 2 * H, ACT.Sigmoid)
+        activate(3 * H, 4 * H, ACT.Tanh)
+        activate(2 * H, 3 * H, ACT.Sigmoid)
+        m = mask_f32[:, 0:1]
+        fcm = keep.tile([P, H], F32)
+        nc.vector.scalar_tensor_tensor(
+            out=fcm[:], in0=gates[:, H : 2 * H], scalar=m, in1=c_prev[:],
+            op0=ALU.mult, op1=ALU.mult,
+        )
+        ig = keep.tile([P, H], F32)
+        nc.vector.tensor_tensor(
+            out=ig[:], in0=gates[:, 0:H], in1=gates[:, 3 * H : 4 * H], op=ALU.mult
+        )
+        c_t = keep.tile([P, H], F32)
+        nc.vector.scalar_tensor_tensor(
+            out=c_t[:], in0=ig[:], scalar=m, in1=fcm[:], op0=ALU.mult, op1=ALU.add
+        )
+        nc.sync.dma_start(out=out_1, in_=c_t[:])
+        tanh_c = keep.tile([P, H], F32)
+        nc.scalar.activation(out=tanh_c[:], in_=c_t[:], func=ACT.Tanh)
+        tc_m = keep.tile([P, H], F32)
+        nc.vector.tensor_scalar(
+            out=tc_m[:], in0=tanh_c[:], scalar1=m, scalar2=None, op0=ALU.mult
+        )
+        h_new = keep.tile([P, H], F32)
+        nc.vector.tensor_tensor(
+            out=h_new[:], in0=gates[:, 2 * H : 3 * H], in1=tc_m[:], op=ALU.mult
+        )
+        nc.sync.dma_start(out=out_0, in_=h_new[:])
+
+        for n in range(PASSES, len(pieces)):
+            multiply_and_load_ahead(n)
+
+        for b in SHARE_BANKS:
+            add_plain_sum(b)
+        for b in SHARE_BANKS:
+            first, last = bank_columns(range(b, b + 1))
+            activate(first, last, ACT.Sigmoid)
+        s0 = keep.tile([P, H], F32)
+        nc.vector.tensor_tensor(out=s0[:], in0=gates[:, 4 * H : 5 * H], in1=tc_m[:], op=ALU.mult)
+        nc.sync.dma_start(out=out_2, in_=s0[:])
+        s1 = keep.tile([P, H], F32)
+        cut = SHARE_BANKS[-1] * BANK - 5 * H
+        nc.vector.tensor_tensor(
+            out=s1[:, 0:cut], in0=gates[:, 5 * H : 5 * H + cut], in1=tc_m[:, 0:cut], op=ALU.mult
+        )
+        nc.vector.tensor_tensor(
+            out=s1[:, cut:H], in0=gates[:, 5 * H + cut : 6 * H], in1=tc_m[:, cut:H], op=ALU.mult
+        )
+        nc.sync.dma_start(out=out_3, in_=s1[:])

@@ -87,6 +87,15 @@ def tile_share_lstm_cell_w_kernel(
         nc.gpsimd.dma_start(
             out=bias_rows[1:2, N_CELL:N_ALL], in_=bias_sh.rearrange("(o n) -> o n", o=1)
         )
+        for tile_no in range(PASSES // PLANES_PER_TILE):
+            g0 = tile_no * PLANES_PER_TILE
+            for quad in range(4):
+                nc.gpsimd.dma_start(
+                    out=w_planes[32 * quad : 32 * quad + 16, tile_no, :].bitcast(F32),
+                    in_=weight_ih_scales[
+                        g0 : g0 + PLANES_PER_TILE, 4 * quad : 4 * quad + 4, :
+                    ].bitcast(F32),
+                )
         c_prev = keep.tile([P, H], BF16)
         nc.gpsimd.dma_start(out=c_prev[:], in_=c_minors)
         mask_bf16 = keep.tile([P, 1], BF16)
@@ -110,16 +119,6 @@ def tile_share_lstm_cell_w_kernel(
                 out=w_raw[:, first // P : last // P, :],
                 in_=rows.rearrange("(p j) k -> p j k", j=rows_each),
             )
-
-        for tile_no in range(PASSES // PLANES_PER_TILE):
-            g0 = tile_no * PLANES_PER_TILE
-            for quad in range(4):
-                nc.sync.dma_start(
-                    out=w_planes[32 * quad : 32 * quad + 16, tile_no, :].bitcast(I32),
-                    in_=weight_ih_scales[
-                        g0 : g0 + PLANES_PER_TILE, 4 * quad : 4 * quad + 4, :
-                    ].bitcast(I32),
-                )
 
         whole = range(PASSES - SPLIT_PASSES)
         split = range(PASSES - SPLIT_PASSES, PASSES)

@@ -27,7 +27,8 @@ SHARE_BANKS = range(3, 5)
 PLANES_PER_TILE = 4
 X_PIECES = 4
 PASSES_PER_PIECE = PASSES // X_PIECES
-SPLIT_PASSES = 6
+SPLIT_PASSES = 10
+TAPER_PASSES = 4
 W_BUFS = 11
 
 FLOPS = 2 * P * (D_IN * N_ALL + H * N_ALL)
@@ -87,6 +88,10 @@ def tile_share_lstm_cell_w_kernel(
         nc.gpsimd.dma_start(
             out=bias_rows[1:2, N_CELL:N_ALL], in_=bias_sh.rearrange("(o n) -> o n", o=1)
         )
+        c_prev = keep.tile([P, H], BF16)
+        nc.gpsimd.dma_start(out=c_prev[:], in_=c_minors)
+        mask_bf16 = keep.tile([P, 1], BF16)
+        nc.gpsimd.dma_start(out=mask_bf16[:], in_=mask.rearrange("(p o) -> p o", o=1))
         for tile_no in range(PASSES // PLANES_PER_TILE):
             g0 = tile_no * PLANES_PER_TILE
             for quad in range(4):
@@ -96,10 +101,6 @@ def tile_share_lstm_cell_w_kernel(
                         g0 : g0 + PLANES_PER_TILE, 4 * quad : 4 * quad + 4, :
                     ].bitcast(F32),
                 )
-        c_prev = keep.tile([P, H], BF16)
-        nc.gpsimd.dma_start(out=c_prev[:], in_=c_minors)
-        mask_bf16 = keep.tile([P, 1], BF16)
-        nc.gpsimd.dma_start(out=mask_bf16[:], in_=mask.rearrange("(p o) -> p o", o=1))
 
         x_sb = keep.tile([P, D_IN], BF16)
         x_cols = D_IN // X_PIECES
@@ -122,9 +123,12 @@ def tile_share_lstm_cell_w_kernel(
 
         whole = range(PASSES - SPLIT_PASSES)
         split = range(PASSES - SPLIT_PASSES, PASSES)
+        taper = range(PASSES - TAPER_PASSES, PASSES)
         pieces = [(g, ALL_BANKS) for g in whole]
         pieces += [(g, CELL_BANKS) for g in split]
-        pieces += [(g, SHARE_BANKS) for g in split]
+        pieces += [(g, SHARE_BANKS) for g in split if g not in taper]
+        pieces += [(g, SHARE_BANKS[:1]) for g in taper]
+        pieces += [(g, SHARE_BANKS[1:]) for g in taper]
         w_words = {}
 
         def load_piece(g, banks):
@@ -140,7 +144,9 @@ def tile_share_lstm_cell_w_kernel(
                 .bitcast(I32),
             )
 
-        for g, banks in pieces[:W_BUFS]:
+        opening = pieces[:PASSES]
+        late = pieces[PASSES:]
+        for g, banks in opening[:W_BUFS]:
             load_piece(g, banks)
 
         x_words = x_sb[:].bitcast(F32)
@@ -265,13 +271,13 @@ def tile_share_lstm_cell_w_kernel(
         def activate(first, last, func):
             nc.scalar.activation(out=gates[:, first:last], in_=gates[:, first:last], func=func)
 
-        def multiply_and_load_ahead(n):
-            multiply_piece(*pieces[n])
-            if n + W_BUFS < len(pieces):
-                load_piece(*pieces[n + W_BUFS])
-
-        for n in range(PASSES):
-            multiply_and_load_ahead(n)
+        for n in range(PASSES - W_BUFS):
+            multiply_piece(*opening[n])
+            load_piece(*opening[n + W_BUFS])
+        for g, banks in late:
+            load_piece(g, banks)
+        for g, banks in opening[PASSES - W_BUFS :]:
+            multiply_piece(g, banks)
 
         for b in CELL_BANKS:
             add_plain_sum(b)
@@ -295,33 +301,34 @@ def tile_share_lstm_cell_w_kernel(
         nc.sync.dma_start(out=out_1, in_=c_t[:])
         tanh_c = keep.tile([P, H], F32)
         nc.scalar.activation(out=tanh_c[:], in_=c_t[:], func=ACT.Tanh)
-        tc_m = keep.tile([P, H], F32)
-        nc.vector.tensor_scalar(
-            out=tc_m[:], in0=tanh_c[:], scalar1=m, scalar2=None, op0=ALU.mult
-        )
+        tc_twice = keep.tile([P, 2, H], F32)
+        for share in range(2):
+            nc.vector.tensor_scalar(
+                out=tc_twice[:, share, :], in0=tanh_c[:], scalar1=m, scalar2=None, op0=ALU.mult
+            )
         h_new = keep.tile([P, H], F32)
         nc.vector.tensor_tensor(
-            out=h_new[:], in0=gates[:, 2 * H : 3 * H], in1=tc_m[:], op=ALU.mult
+            out=h_new[:], in0=gates[:, 2 * H : 3 * H], in1=tc_twice[:, 0, :], op=ALU.mult
         )
         nc.sync.dma_start(out=out_0, in_=h_new[:])
 
-        for n in range(PASSES, len(pieces)):
-            multiply_and_load_ahead(n)
+        for g, banks in late:
+            multiply_piece(g, banks)
 
         for b in SHARE_BANKS:
             add_plain_sum(b)
         for b in SHARE_BANKS:
             first, last = bank_columns(range(b, b + 1))
             activate(first, last, ACT.Sigmoid)
-        s0 = keep.tile([P, H], F32)
-        nc.vector.tensor_tensor(out=s0[:], in0=gates[:, 4 * H : 5 * H], in1=tc_m[:], op=ALU.mult)
-        nc.sync.dma_start(out=out_2, in_=s0[:])
-        s1 = keep.tile([P, H], F32)
-        cut = SHARE_BANKS[-1] * BANK - 5 * H
-        nc.vector.tensor_tensor(
-            out=s1[:, 0:cut], in0=gates[:, 5 * H : 5 * H + cut], in1=tc_m[:, 0:cut], op=ALU.mult
-        )
-        nc.vector.tensor_tensor(
-            out=s1[:, cut:H], in0=gates[:, 5 * H + cut : 6 * H], in1=tc_m[:, cut:H], op=ALU.mult
-        )
-        nc.sync.dma_start(out=out_3, in_=s1[:])
+        s_both = keep.tile([P, 2 * H], F32)
+        tc_flat = tc_twice[:].rearrange("p s h -> p (s h)")
+        for b in SHARE_BANKS:
+            first, last = bank_columns(range(b, b + 1))
+            nc.vector.tensor_tensor(
+                out=s_both[:, first - N_CELL : last - N_CELL],
+                in0=gates[:, first:last],
+                in1=tc_flat[:, first - N_CELL : last - N_CELL],
+                op=ALU.mult,
+            )
+        nc.sync.dma_start(out=out_2, in_=s_both[:, 0:H])
+        nc.sync.dma_start(out=out_3, in_=s_both[:, H : 2 * H])

@@ -92,15 +92,18 @@ def tile_share_lstm_cell_w_kernel(
         nc.gpsimd.dma_start(out=c_prev[:], in_=c_minors)
         mask_bf16 = keep.tile([P, 1], BF16)
         nc.gpsimd.dma_start(out=mask_bf16[:], in_=mask.rearrange("(p o) -> p o", o=1))
-        for tile_no in range(PASSES // PLANES_PER_TILE):
+        def load_planes(queue, tile_no, quad):
             g0 = tile_no * PLANES_PER_TILE
-            for quad in range(4):
-                nc.gpsimd.dma_start(
-                    out=w_planes[32 * quad : 32 * quad + 16, tile_no, :].bitcast(F32),
-                    in_=weight_ih_scales[
-                        g0 : g0 + PLANES_PER_TILE, 4 * quad : 4 * quad + 4, :
-                    ].bitcast(F32),
-                )
+            queue.dma_start(
+                out=w_planes[32 * quad : 32 * quad + 16, tile_no, :].bitcast(F32),
+                in_=weight_ih_scales[
+                    g0 : g0 + PLANES_PER_TILE, 4 * quad : 4 * quad + 4, :
+                ].bitcast(F32),
+            )
+
+        for tile_no in range(PASSES // PLANES_PER_TILE):
+            for quad in (2, 3):
+                load_planes(nc.gpsimd, tile_no, quad)
 
         x_sb = keep.tile([P, D_IN], BF16)
         x_cols = D_IN // X_PIECES
@@ -146,8 +149,11 @@ def tile_share_lstm_cell_w_kernel(
 
         opening = pieces[:PASSES]
         late = pieces[PASSES:]
-        for g, banks in opening[:W_BUFS]:
-            load_piece(g, banks)
+        for n in range(W_BUFS):
+            if n % 2 == 0 and n // 2 < PASSES // PLANES_PER_TILE:
+                for quad in (0, 1):
+                    load_planes(nc.sync, n // 2, quad)
+            load_piece(*opening[n])
 
         x_words = x_sb[:].bitcast(F32)
         words_per_pass = K_PASS // 2

@@ -27,7 +27,7 @@ SHARE_BANKS = range(3, 5)
 PLANES_PER_TILE = 4
 X_PIECES = 4
 PASSES_PER_PIECE = PASSES // X_PIECES
-SPLIT_PASSES = 10
+SPLIT_PASSES = 8
 TAPER_PASSES = 4
 W_BUFS = 11
 
@@ -73,7 +73,7 @@ def tile_share_lstm_cell_w_kernel(
         nc.vector.memset(ones[:], 1.0)
 
         bias_rows = keep.tile([P, N_ALL], BF16)
-        nc.vector.memset(bias_rows[:], 0.0)
+        nc.vector.memset(bias_rows[:].bitcast(I32), 0)
 
         w_planes = keep.tile([P, PASSES // PLANES_PER_TILE, N_ALL], U8, align_bytes=64)
         nc.vector.memset(w_planes[:].bitcast(I32), 0)
@@ -106,22 +106,18 @@ def tile_share_lstm_cell_w_kernel(
                 load_planes(nc.gpsimd, tile_no, quad)
 
         x_sb = keep.tile([P, D_IN], BF16)
-        x_cols = D_IN // X_PIECES
-        for piece in range(X_PIECES):
-            cols = slice(piece * x_cols, (piece + 1) * x_cols)
-            nc.sync.dma_start(out=x_sb[:, cols], in_=x[:, cols])
+        nc.sync.dma_start(out=x_sb[:], in_=x)
 
         w_raw = keep.tile([P, N_ALL // P, H], BF16)
-        for b in ALL_BANKS:
-            first, last = bank_columns(range(b, b + 1))
-            rows_each = (last - first) // P
-            if last <= N_CELL:
-                rows = weight_hh[first:last, :]
-            else:
-                rows = weight_sh[first - N_CELL : last - N_CELL, :]
+        cell_slots = N_CELL // P
+        share_slots = N_ALL // P - cell_slots
+        for rows, slots in (
+            (weight_hh, slice(0, cell_slots)),
+            (weight_sh, slice(cell_slots, cell_slots + share_slots)),
+        ):
             nc.sync.dma_start(
-                out=w_raw[:, first // P : last // P, :],
-                in_=rows.rearrange("(p j) k -> p j k", j=rows_each),
+                out=w_raw[:, slots, :],
+                in_=rows.rearrange("(p j) k -> p j k", j=slots.stop - slots.start),
             )
 
         whole = range(PASSES - SPLIT_PASSES)
@@ -222,7 +218,27 @@ def tile_share_lstm_cell_w_kernel(
                     in_=block_t[:].rearrange("k j p -> k p j"),
                 )
 
+        def columns_of_batch(row, b):
+            first, last = bank_columns(range(b, b + 1))
+            slot, end = first // P, last // P
+            if last <= N_CELL:
+                part = row[:, 0:N_CELL].rearrange("r (p j) -> r p j", j=cell_slots)
+                return part[:, :, slot:end]
+            part = row[:, N_CELL:N_ALL].rearrange("r (p j) -> r p j", j=share_slots)
+            return part[:, :, slot - cell_slots : end - cell_slots]
+
         plain_sum = keep.tile([P, N_ALL], F32)
+        bias_batches = keep.tile([P, N_ALL], BF16)
+
+        def order_biases():
+            for b in ALL_BANKS:
+                first, last = bank_columns(range(b, b + 1))
+                nc.vector.tensor_copy(
+                    out=bias_batches[:, first:last].rearrange(
+                        "r (p j) -> r p j", j=(last - first) // P
+                    ),
+                    in_=columns_of_batch(bias_rows, b),
+                )
 
         def plain_products(b):
             first, last = bank_columns(range(b, b + 1))
@@ -234,11 +250,16 @@ def tile_share_lstm_cell_w_kernel(
                     start=(kc == 0), stop=False,
                 )
             nc.tensor.matmul(
-                plain_ps[:], lhsT=ones[:], rhs=bias_rows[:, first:last], start=False, stop=True
+                plain_ps[:], lhsT=ones[:], rhs=bias_batches[:, first:last], start=False, stop=True
             )
-            copy_out(nc, b, out=plain_sum[:, first:last], in_=plain_ps[:])
+            copy_out(
+                nc, b,
+                out=columns_of_batch(plain_sum, b),
+                in_=plain_ps[:].rearrange("r (p j) -> r p j", j=(last - first) // P),
+            )
 
         transpose_plain_weights(0)
+        order_biases()
         for b in ALL_BANKS:
             if b + 1 < len(ALL_BANKS):
                 transpose_plain_weights(b + 1)
@@ -287,9 +308,10 @@ def tile_share_lstm_cell_w_kernel(
 
         for b in CELL_BANKS:
             add_plain_sum(b)
-        activate(0, 2 * H, ACT.Sigmoid)
+        activate(0, BANK, ACT.Sigmoid)
+        activate(BANK, 2 * BANK, ACT.Sigmoid)
         activate(3 * H, 4 * H, ACT.Tanh)
-        activate(2 * H, 3 * H, ACT.Sigmoid)
+        activate(2 * BANK, 3 * H, ACT.Sigmoid)
         m = mask_f32[:, 0:1]
         fcm = keep.tile([P, H], F32)
         nc.vector.scalar_tensor_tensor(

from contextlib import ExitStack

import concourse.mybir as mybir
from concourse.masks import make_identity

F32 = mybir.dt.float32
BF16 = mybir.dt.bfloat16
I32 = mybir.dt.int32
U32 = mybir.dt.uint32
U8 = mybir.dt.uint8
FP8X4 = mybir.dt.float8_e4m3fn_x4
ACT = mybir.ActivationFunctionType
ALU = mybir.AluOpType

P = 128
D_IN = 8192
H = 384
N_CELL = 4 * H
N_ALL = 6 * H
K_PASS = 4 * P
PASSES = D_IN // K_PASS
H_CHUNKS = H // P
BANK = 512
ALL_BANKS = range(0, 5)
CELL_BANKS = range(0, 3)
SHARE_BANKS = range(3, 5)
PLANES_PER_TILE = 4
X_PIECES = 4
PASSES_PER_PIECE = PASSES // X_PIECES
SPLIT_PASSES = 8
TAPER_PASSES = 4
W_BUFS = 11

FLOPS = 2 * P * (D_IN * N_ALL + H * N_ALL)
BYTES = (
    2 * P * D_IN + 3 * 2 * P * H + 2 * P + D_IN * N_ALL + D_IN // 32 * N_ALL
    + 2 * N_ALL * H + 2 * 2 * N_ALL + 4 * 4 * P * H
)


def bank_columns(banks):
    return banks[0] * BANK, min((banks[-1] + 1) * BANK, N_ALL)


def copy_out(nc, turn, out, in_):
    if turn % 2 == 0:
        nc.vector.tensor_copy(out=out, in_=in_)
    else:
        nc.scalar.copy(out=out, in_=in_)


def tile_share_lstm_cell_w_kernel(
    tc, x, h_minors, c_minors, s_minors, mask, weight_ih_words, weight_ih_scales,
    weight_hh, weight_sh, bias_ih, bias_hh, bias_sh, idx, out_0, out_1, out_2, out_3,
):
    nc = tc.nc
    with ExitStack() as stack:
        keep = stack.enter_context(tc.tile_pool(name="keep", bufs=1))
        w_pool = stack.enter_context(tc.tile_pool(name="w_pool", bufs=W_BUFS))
        acc_pool = stack.enter_context(tc.psum_pool(name="acc_pool", bufs=1))
        work = stack.enter_context(tc.psum_pool(name="work", bufs=3))
        stack.enter_context(tc.manual_schedule())

        warm = keep.tile([P, 1], F32)
        nc.vector.memset(warm[:], 0.0)
        nc.scalar.activation(out=warm[:], in_=warm[:], func=ACT.Sigmoid)

        ident_f32 = keep.tile([P, P], F32)
        make_identity(nc, ident_f32[:])
        ident_bf16 = keep.tile([P, P], BF16)
        make_identity(nc, ident_bf16[:])
        ones = keep.tile([P, P], BF16)
        nc.vector.memset(ones[:], 1.0)

        bias_rows = keep.tile([P, N_ALL], BF16)
        nc.vector.memset(bias_rows[:].bitcast(I32), 0)

        w_planes = keep.tile([P, PASSES // PLANES_PER_TILE, N_ALL], U8, align_bytes=64)
        nc.vector.memset(w_planes[:].bitcast(I32), 0)

        hs_raw = keep.tile([P, 2, H], BF16)
        nc.gpsimd.dma_start(out=hs_raw[:, 0, :], in_=h_minors)
        nc.gpsimd.dma_start(out=hs_raw[:, 1, :], in_=s_minors[idx])
        nc.gpsimd.dma_start(out=bias_rows[0:1, :], in_=bias_ih.rearrange("(o n) -> o n", o=1))
        nc.gpsimd.dma_start(
            out=bias_rows[1:2, 0:N_CELL], in_=bias_hh.rearrange("(o n) -> o n", o=1)
        )
        nc.gpsimd.dma_start(
            out=bias_rows[1:2, N_CELL:N_ALL], in_=bias_sh.rearrange("(o n) -> o n", o=1)
        )
        c_prev = keep.tile([P, H], BF16)
        nc.gpsimd.dma_start(out=c_prev[:], in_=c_minors)
        mask_bf16 = keep.tile([P, 1], BF16)
        nc.gpsimd.dma_start(out=mask_bf16[:], in_=mask.rearrange("(p o) -> p o", o=1))
        def load_planes(queue, tile_no, quad):
            g0 = tile_no * PLANES_PER_TILE
            queue.dma_start(
                out=w_planes[32 * quad : 32 * quad + 16, tile_no, :].bitcast(F32),
                in_=weight_ih_scales[
                    g0 : g0 + PLANES_PER_TILE, 4 * quad : 4 * quad + 4, :
                ].bitcast(F32),
            )

        for tile_no in range(PASSES // PLANES_PER_TILE):
            for quad in (2, 3):
                load_planes(nc.gpsimd, tile_no, quad)

        x_sb = keep.tile([P, D_IN], BF16)
        nc.sync.dma_start(out=x_sb[:], in_=x)

        w_raw = keep.tile([P, N_ALL // P, H], BF16)
        cell_slots = N_CELL // P
        share_slots = N_ALL // P - cell_slots
        for rows, slots in (
            (weight_hh, slice(0, cell_slots)),
            (weight_sh, slice(cell_slots, cell_slots + share_slots)),
        ):
            nc.sync.dma_start(
                out=w_raw[:, slots, :],
                in_=rows.rearrange("(p j) k -> p j k", j=slots.stop - slots.start),
            )

        whole = range(PASSES - SPLIT_PASSES)
        split = range(PASSES - SPLIT_PASSES, PASSES)
        taper = range(PASSES - TAPER_PASSES, PASSES)
        pieces = [(g, ALL_BANKS) for g in whole]
        pieces += [(g, CELL_BANKS) for g in split]
        pieces += [(g, SHARE_BANKS) for g in split if g not in taper]
        pieces += [(g, SHARE_BANKS[:1]) for g in taper]
        pieces += [(g, SHARE_BANKS[1:]) for g in taper]
        w_words = {}

        def load_piece(g, banks):
            if g not in w_words:
                w_words[g] = w_pool.tile(
                    [P, N_ALL], U32, name="w_words_%d" % g, tag="w_words", align_bytes=64
                )
            first, last = bank_columns(banks)
            nc.sync.dma_start(
                out=w_words[g][:, first:last].bitcast(I32),
                in_=weight_ih_words[g]
                .rearrange("p n t -> p (n t)")[:, 4 * first : 4 * last]
                .bitcast(I32),
            )

        opening = pieces[:PASSES]
        late = pieces[PASSES:]
        for n in range(W_BUFS):
            if n % 2 == 0 and n // 2 < PASSES // PLANES_PER_TILE:
                for quad in (0, 1):
                    load_planes(nc.sync, n // 2, quad)
            load_piece(*opening[n])

        x_words = x_sb[:].bitcast(F32)
        words_per_pass = K_PASS // 2
        x_grouped = keep.tile([P, PASSES * P * 4], BF16, align_bytes=64)
        x_grouped_words = x_grouped[:].bitcast(F32).rearrange(
            "p (g r u) -> p g r u", g=PASSES, u=2
        )
        x_codes = keep.tile([P, PASSES * P], U32, align_bytes=64)
        x_scales = keep.tile([P, PASSES * P], U8, align_bytes=64)

        def quantise_piece(piece):
            first = piece * PASSES_PER_PIECE * P
            last = first + PASSES_PER_PIECE * P
            nc.vector.quantize_mx(
                out=x_codes[:, first:last].bitcast(FP8X4),
                scales=x_scales[:, first:last],
                in_=x_grouped[:, 4 * first : 4 * last],
            )

        for piece in range(X_PIECES):
            for half in range(PASSES_PER_PIECE // 2):
                g0 = piece * PASSES_PER_PIECE + 2 * half
                x_t = work.tile([P, 2, 2, P], F32, tag="work")
                for i in range(2):
                    for u in range(2):
                        start_word = (g0 + i) * words_per_pass
                        nc.tensor.transpose(
                            x_t[:, i, u, :],
                            x_words[:, start_word + u : start_word + words_per_pass : 2],
                            ident_f32[:],
                        )
                copy_out(
                    nc, half,
                    out=x_grouped_words[:, g0 : g0 + 2, :, :],
                    in_=x_t[:].rearrange("p i u r -> p i r u"),
                )
            if piece > 0:
                quantise_piece(piece - 1)
        quantise_piece(X_PIECES - 1)

        hs_t = keep.tile([P, 2, H_CHUNKS, P], BF16)
        for side in range(2):
            h_t = work.tile([P, H_CHUNKS, P], BF16, tag="work")
            for kc in range(H_CHUNKS):
                nc.tensor.transpose(
                    h_t[:, kc, :], hs_raw[:, side, kc * P : (kc + 1) * P], ident_bf16[:]
                )
            copy_out(nc, side, out=hs_t[:, side, :, :], in_=h_t[:])

        w_t = keep.tile([P, H_CHUNKS, N_ALL], BF16)

        def transpose_plain_weights(b):
            first, last = bank_columns(range(b, b + 1))
            rows_each = (last - first) // P
            for kc in range(H_CHUNKS):
                block_t = work.tile([P, rows_each, P], BF16, tag="work")
                for j in range(rows_each):
                    nc.tensor.transpose(
                        block_t[:, j, :],
                        w_raw[:, first // P + j, kc * P : (kc + 1) * P],
                        ident_bf16[:],
                    )
                copy_out(
                    nc, b + kc,
                    out=w_t[:, kc, first:last].rearrange("k (p j) -> k p j", j=rows_each),
                    in_=block_t[:].rearrange("k j p -> k p j"),
                )

        def columns_of_batch(row, b):
            first, last = bank_columns(range(b, b + 1))
            slot, end = first // P, last // P
            if last <= N_CELL:
                part = row[:, 0:N_CELL].rearrange("r (p j) -> r p j", j=cell_slots)
                return part[:, :, slot:end]
            part = row[:, N_CELL:N_ALL].rearrange("r (p j) -> r p j", j=share_slots)
            return part[:, :, slot - cell_slots : end - cell_slots]

        plain_sum = keep.tile([P, N_ALL], F32)
        bias_batches = keep.tile([P, N_ALL], BF16)

        def order_biases():
            for b in ALL_BANKS:
                first, last = bank_columns(range(b, b + 1))
                nc.vector.tensor_copy(
                    out=bias_batches[:, first:last].rearrange(
                        "r (p j) -> r p j", j=(last - first) // P
                    ),
                    in_=columns_of_batch(bias_rows, b),
                )

        def plain_products(b):
            first, last = bank_columns(range(b, b + 1))
            side = 0 if last <= N_CELL else 1
            plain_ps = work.tile([P, last - first], F32, tag="work")
            for kc in range(H_CHUNKS):
                nc.tensor.matmul(
                    plain_ps[:], lhsT=hs_t[:, side, kc, :], rhs=w_t[:, kc, first:last],
                    start=(kc == 0), stop=False,
                )
            nc.tensor.matmul(
                plain_ps[:], lhsT=ones[:], rhs=bias_batches[:, first:last], start=False, stop=True
            )
            copy_out(
                nc, b,
                out=columns_of_batch(plain_sum, b),
                in_=plain_ps[:].rearrange("r (p j) -> r p j", j=(last - first) // P),
            )

        transpose_plain_weights(0)
        order_biases()
        for b in ALL_BANKS:
            if b + 1 < len(ALL_BANKS):
                transpose_plain_weights(b + 1)
            plain_products(b)

        mask_f32 = keep.tile([P, 1], F32)
        nc.vector.tensor_copy(out=mask_f32[:], in_=mask_bf16[:])

        acc = []
        for b in ALL_BANKS:
            first, last = bank_columns(range(b, b + 1))
            acc.append(acc_pool.tile([P, last - first], F32, name="acc%d" % b))

        def multiply_piece(g, banks):
            offset = 4 * (g % PLANES_PER_TILE)
            for b in banks:
                first, last = bank_columns(range(b, b + 1))
                nc.tensor.matmul_mx(
                    out=acc[b][:],
                    lhsT=x_codes[:, g * P : (g + 1) * P].bitcast(FP8X4),
                    lhsT_scale=x_scales[:, g * P : (g + 1) * P],
                    rhs=w_words[g][:, first:last].bitcast(FP8X4),
                    rhs_scale=w_planes[offset:P, g // PLANES_PER_TILE, first:last],
                    start=(g == 0),
                    stop=(g == PASSES - 1),
                )

        gates = keep.tile([P, N_ALL], F32)

        def add_plain_sum(b):
            first, last = bank_columns(range(b, b + 1))
            nc.vector.tensor_tensor(
                out=gates[:, first:last], in0=acc[b][:], in1=plain_sum[:, first:last], op=ALU.add
            )

        def activate(first, last, func):
            nc.scalar.activation(out=gates[:, first:last], in_=gates[:, first:last], func=func)

        for n in range(PASSES - W_BUFS):
            multiply_piece(*opening[n])
            load_piece(*opening[n + W_BUFS])
        for g, banks in late:
            load_piece(g, banks)
        for g, banks in opening[PASSES - W_BUFS :]:
            multiply_piece(g, banks)

        for b in CELL_BANKS:
            add_plain_sum(b)
        activate(0, BANK, ACT.Sigmoid)
        activate(BANK, 2 * BANK, ACT.Sigmoid)
        activate(3 * H, 4 * H, ACT.Tanh)
        activate(2 * BANK, 3 * H, ACT.Sigmoid)
        m = mask_f32[:, 0:1]
        fcm = keep.tile([P, H], F32)
        nc.vector.scalar_tensor_tensor(
            out=fcm[:], in0=gates[:, H : 2 * H], scalar=m, in1=c_prev[:],
            op0=ALU.mult, op1=ALU.mult,
        )
        ig = keep.tile([P, H], F32)
        nc.vector.tensor_tensor(
            out=ig[:], in0=gates[:, 0:H], in1=gates[:, 3 * H : 4 * H], op=ALU.mult
        )
        c_t = keep.tile([P, H], F32)
        nc.vector.scalar_tensor_tensor(
            out=c_t[:], in0=ig[:], scalar=m, in1=fcm[:], op0=ALU.mult, op1=ALU.add
        )
        nc.sync.dma_start(out=out_1, in_=c_t[:])
        tanh_c = keep.tile([P, H], F32)
        nc.scalar.activation(out=tanh_c[:], in_=c_t[:], func=ACT.Tanh)
        tc_twice = keep.tile([P, 2, H], F32)
        for share in range(2):
            nc.vector.tensor_scalar(
                out=tc_twice[:, share, :], in0=tanh_c[:], scalar1=m, scalar2=None, op0=ALU.mult
            )
        h_new = keep.tile([P, H], F32)
        nc.vector.tensor_tensor(
            out=h_new[:], in0=gates[:, 2 * H : 3 * H], in1=tc_twice[:, 0, :], op=ALU.mult
        )
        nc.sync.dma_start(out=out_0, in_=h_new[:])

        for g, banks in late:
            multiply_piece(g, banks)

        for b in SHARE_BANKS:
            add_plain_sum(b)
        for b in SHARE_BANKS:
            first, last = bank_columns(range(b, b + 1))
            activate(first, last, ACT.Sigmoid)
        s_both = keep.tile([P, 2 * H], F32)
        tc_flat = tc_twice[:].rearrange("p s h -> p (s h)")
        for b in SHARE_BANKS:
            first, last = bank_columns(range(b, b + 1))
            nc.vector.tensor_tensor(
                out=s_both[:, first - N_CELL : last - N_CELL],
                in0=gates[:, first:last],
                in1=tc_flat[:, first - N_CELL : last - N_CELL],
                op=ALU.mult,
            )
        nc.sync.dma_start(out=out_2, in_=s_both[:, 0:H])
        nc.sync.dma_start(out=out_3, in_=s_both[:, H : 2 * H])
